import numpy as np
import ml_dtypes


def mxq(x, axis, fmt="e4m3"):
    dtype, down = {"e4m3": (ml_dtypes.float8_e4m3fn, 7), "e5m2": (ml_dtypes.float8_e5m2, 14)}[fmt]
    v = np.moveaxis(np.asarray(x, np.float32).astype(ml_dtypes.bfloat16).astype(np.float64), axis, -1)
    blocks = v.reshape(v.shape[:-1] + (-1, 32))
    amax = np.abs(blocks).max(-1, keepdims=True)
    byte = np.maximum(np.where(amax > 0, np.frexp(amax)[1] - 1 + 127, 0) - down, 1)
    scale = np.exp2(byte - 127.0)
    codes = (blocks / scale).astype(np.float32).astype(dtype).astype(np.float64)
    return np.moveaxis((codes * scale).reshape(v.shape), -1, axis)


WIDE = False


def mx_kscale(k):
    if not WIDE:
        return np.ones(k)
    levels = np.array([10, -10, 5, -5, 0])
    if k % 512:
        return np.exp2(np.random.permutation(np.resize(levels, k // 32))).repeat(32)
    a = np.empty((k // 512, 16))
    for p in range(k // 512):
        a[p, :8] = np.random.permutation(np.resize(levels, 8))
        for g in range(8):
            far = levels[np.abs(levels - a[p, g]) >= 10]
            a[p, g + 8] = far[np.random.randint(len(far))]
    return np.exp2(a.ravel()).repeat(32)


BF16 = ml_dtypes.bfloat16


def bf(x):
    return np.asarray(x, np.float32).astype(BF16)


def f64(x):
    return np.asarray(x).astype(np.float64)


B, F, O = 1024, 2048, 1024


def setup_inputs():
    s = mx_kscale(F)
    return {"x": bf(np.random.standard_normal((B, 2, F)) * s),
            "filters_real": bf(np.random.standard_normal((O, F)) * 0.5 / np.sqrt(F) / s),
            "filters_imag": bf(np.random.standard_normal((O, F)) * 0.5 / np.sqrt(F) / s)}


def reference(x, filters_real, filters_imag):
    x = f64(x)
    x_real = x[:, 0]
    x_imag = x[:, 1]
    w_r = f64(filters_real) + f64(filters_imag)
    w_i = f64(filters_real) - f64(filters_imag)
    energies = (mxq(x_real, 1, "e4m3") @ mxq(w_r, 1, "e4m3").T) + (mxq(x_imag, 1, "e4m3") @ mxq(w_i, 1, "e4m3").T)
    return energies

@@ -1,0 +1,162 @@
+from contextlib import ExitStack
+
+import concourse.mybir as mybir
+from concourse.masks import make_identity
+
+F32 = mybir.dt.float32
+BF16 = mybir.dt.bfloat16
+U32 = mybir.dt.uint32
+U8 = mybir.dt.uint8
+FP8X4 = mybir.dt.float8_e4m3fn_x4
+ADD = mybir.AluOpType.add
+SUB = mybir.AluOpType.subtract
+
+P = 128
+B, F, O = 1024, 2048, 1024
+FLOPS = 2 * B * O * 2 * F
+PASSES = 8
+NCOL = 256
+
+UNITS = (
+    ("W", 0), ("W", 1), ("X", 0), ("X", 1), ("X", 2), ("X", 3), ("W", 2), ("W", 3),
+    ("X", 4), ("X", 5), ("X", 6), ("X", 7), ("W", 4), ("W", 5), ("W", 6), ("W", 7),
+)
+LAG_W = 3
+LAG_X = 3
+RAW_BUFS = 6
+STAGE_BUFS = 8
+WARM_FIRST = 6
+WARM_EACH = 2
+WARM_UNITS = 6
+
+
+def pe_sequence():
+    pos = {}
+    for n, u in enumerate(UNITS):
+        pos[u] = n
+    items = []
+    for j in range(O // NCOL):
+        for i in range(B // P):
+            avail = max(pos[("X", i)] + LAG_X, pos[("W", 2 * j)] + LAG_W, pos[("W", 2 * j + 1)] + LAG_W)
+            items.append((avail, j, i))
+    items = sorted(items)
+    seq = []
+    for n in range(len(UNITS)):
+        seq.append(("T", n, 0))
+        if items and items[0][0] <= n:
+            seq.append(("M", items[0][2], items[0][1]))
+            items = items[1:]
+    for it in items:
+        seq.append(("M", it[2], it[1]))
+    return seq
+
+
+def tile_fftmlp_kernel(tc, x, filters_real, filters_imag, out):
+    nc = tc.nc
+    with ExitStack() as ctx:
+        keep = ctx.enter_context(tc.tile_pool(name="keep", bufs=1))
+        raw_pool = ctx.enter_context(tc.tile_pool(name="rawp", bufs=RAW_BUFS))
+        stage_pool = ctx.enter_context(tc.tile_pool(name="stagep", bufs=STAGE_BUFS))
+        wg_pool = ctx.enter_context(tc.tile_pool(name="wgp", bufs=2))
+        res_pool = ctx.enter_context(tc.tile_pool(name="resp", bufs=4))
+        tp_pool = ctx.enter_context(tc.psum_pool(name="tpp", bufs=4))
+        acc_pool = ctx.enter_context(tc.psum_pool(name="accp", bufs=4))
+        ctx.enter_context(tc.manual_schedule())
+
+        warm = keep.tile([P, 512], BF16, name="warm")
+        nc.vector.memset(warm[:], 0.0)
+        ident = keep.tile([P, P], F32, name="ident")
+        make_identity(nc, ident[:])
+
+        x_codes = [keep.tile([P, PASSES * P], U32, name="xc%d" % i, align_bytes=64) for i in range(B // P)]
+        x_scales = [keep.tile([P, PASSES * P], U8, name="xs%d" % i, align_bytes=64) for i in range(B // P)]
+        w_codes = [keep.tile([P, PASSES, NCOL], U32, name="wc%d" % j, align_bytes=64) for j in range(O // NCOL)]
+        w_scales = [keep.tile([P, PASSES, NCOL], U8, name="ws%d" % j, align_bytes=64) for j in range(O // NCOL)]
+
+        raws = {}
+
+        def load(n):
+            kind, idx = UNITS[n]
+            raw = raw_pool.tile([P, 2 * F], BF16, name="raw", tag="raw")
+            rows = slice(idx * P, (idx + 1) * P)
+            if kind == "X":
+                nc.sync.dma_start(out=raw[:], in_=x[rows, :, :].rearrange("m c k -> m (c k)"))
+            else:
+                cuts = 2 if n == 0 else 1
+                step = F // cuts
+                for h in range(cuts):
+                    cols = slice(h * step, (h + 1) * step)
+                    nc.sync.dma_start(out=raw[:, h * step:(h + 1) * step], in_=filters_real[rows, cols])
+                    nc.sync.dma_start(out=raw[:, F + h * step:F + (h + 1) * step], in_=filters_imag[rows, cols])
+            raws[n] = raw
+
+        warm_ps = acc_pool.tile([P, 512], F32, name="warm_ps", tag="acc")
+
+        def warm_up(count):
+            for d in range(count):
+                nc.tensor.matmul(out=warm_ps[:], lhsT=warm[:, 0:P], rhs=warm[:], start=True, stop=True)
+
+        def transpose_unit(n):
+            kind, idx = UNITS[n]
+            words = raws[n][:].bitcast(F32)
+            stage = stage_pool.tile([P, 2 * F], BF16, name="stage", tag="stage", align_bytes=64)
+            stage_words = stage[:].bitcast(F32)
+            for b in range(4):
+                tp = tp_pool.tile([P, 512], F32, name="tp", tag="tp")
+                if kind == "X":
+                    starts = [512 * b, 512 * b + 256]
+                else:
+                    starts = [256 * b, 1024 + 256 * b]
+                for s in range(4):
+                    first = starts[s // 2] + s % 2
+                    nc.tensor.transpose(tp[:, s * P:(s + 1) * P], words[:, first:first + 255:2], ident[:])
+                src = tp[:].rearrange("p (g u m) -> p g m u", g=2, u=2)
+                if kind == "X":
+                    dst = stage_words[:, b * 512:(b + 1) * 512].rearrange("p (g m u) -> p g m u", g=2, u=2)
+                else:
+                    dst = stage_words.rearrange("p (f c m u) -> p f c m u", f=2, c=4, u=2)[:, :, b, :, :]
+                nc.scalar.copy(out=dst, in_=src)
+            if kind == "X":
+                nc.vector.quantize_mx(out=x_codes[idx][:].bitcast(FP8X4), scales=x_scales[idx][:], in_=stage[:])
+            else:
+                wg = wg_pool.tile([P, 2 * F], BF16, name="wg", tag="wg", align_bytes=64)
+                nc.vector.tensor_tensor(out=wg[:, 0:F], in0=stage[:, 0:F], in1=stage[:, F:2 * F], op=ADD)
+                nc.vector.tensor_tensor(out=wg[:, F:2 * F], in0=stage[:, 0:F], in1=stage[:, F:2 * F], op=SUB)
+                cols = slice((idx % 2) * P, (idx % 2 + 1) * P)
+                for g in range(PASSES):
+                    nc.vector.quantize_mx(
+                        out=w_codes[idx // 2][:, g, cols].bitcast(FP8X4),
+                        scales=w_scales[idx // 2][:, g, cols],
+                        in_=wg[:, g * 512:(g + 1) * 512],
+                    )
+
+        def multiply(i, j):
+            acc = acc_pool.tile([P, 512], F32, name="acc", tag="acc")
+            for g in range(PASSES):
+                nc.tensor.matmul_mx(
+                    out=acc[:, 0:NCOL],
+                    lhsT=x_codes[i][:, g * P:(g + 1) * P].bitcast(FP8X4),
+                    lhsT_scale=x_scales[i][:, g * P:(g + 1) * P],
+                    rhs=w_codes[j][:, g, :].bitcast(FP8X4),
+                    rhs_scale=w_scales[j][:, g, :],
+                    start=(g == 0),
+                    stop=(g == PASSES - 1),
+                )
+            res = res_pool.tile([P, NCOL], F32, name="res", tag="res")
+            nc.scalar.copy(out=res[:], in_=acc[:, 0:NCOL])
+            nc.sync.dma_start(out=out[i * P:(i + 1) * P, j * NCOL:(j + 1) * NCOL], in_=res[:])
+
+        for n in range(RAW_BUFS):
+            load(n)
+        loaded = RAW_BUFS
+        warm_up(WARM_FIRST)
+        for step in pe_sequence():
+            if step[0] == "T":
+                transpose_unit(step[1])
+                if step[1] < WARM_UNITS:
+                    warm_up(WARM_EACH)
+                if loaded < len(UNITS):
+                    load(loaded)
+                    loaded += 1
+            else:
+                multiply(step[1], step[2])

@@ -14,41 +14,39 @@ SUB = mybir.AluOpType.subtract
 P = 128
 B, F, O = 1024, 2048, 1024
 FLOPS = 2 * B * O * 2 * F
-PASSES = 8
-NCOL = 256
+KS = 512
+SLICES = F // KS
+PASSES = 2 * SLICES
+HALF = 512
 
-UNITS = (
-    ("W", 0), ("W", 1), ("X", 0), ("X", 1), ("X", 2), ("X", 3), ("W", 2), ("W", 3),
-    ("X", 4), ("X", 5), ("X", 6), ("X", 7), ("W", 4), ("W", 5), ("W", 6), ("W", 7),
+CHUNKS = (
+    ("W", 0, 4, 0, 1), ("X", 0, 4, 0, 1), ("W", 0, 4, 1, 1), ("X", 0, 4, 1, 1),
+    ("W", 0, 2, 2, 2), ("W", 2, 2, 2, 2), ("X", 0, 2, 2, 2), ("X", 2, 2, 2, 2),
+    ("X", 4, 2, 0, 2), ("X", 6, 2, 0, 2), ("X", 4, 2, 2, 2), ("X", 6, 2, 2, 2),
+    ("W", 4, 4, 0, 1), ("W", 4, 4, 1, 1), ("W", 4, 4, 2, 1), ("W", 4, 4, 3, 1),
 )
-LAG_W = 3
-LAG_X = 3
-RAW_BUFS = 6
-STAGE_BUFS = 8
+RAW_BUFS = 10
 WARM_FIRST = 6
 WARM_EACH = 2
-WARM_UNITS = 6
+WARM_CHUNKS = 2
 
 
-def pe_sequence():
-    pos = {}
-    for n, u in enumerate(UNITS):
-        pos[u] = n
-    items = []
-    for j in range(O // NCOL):
+def chunk_of(kind, row, s):
+    for n, (k, r0, rn, s0, sn) in enumerate(CHUNKS):
+        if k == kind and r0 <= row < r0 + rn and s0 <= s < s0 + sn:
+            return n
+
+
+def ready_blocks():
+    blocks = []
+    for h in range(2):
         for i in range(B // P):
-            avail = max(pos[("X", i)] + LAG_X, pos[("W", 2 * j)] + LAG_W, pos[("W", 2 * j + 1)] + LAG_W)
-            items.append((avail, j, i))
-    items = sorted(items)
-    seq = []
-    for n in range(len(UNITS)):
-        seq.append(("T", n, 0))
-        if items and items[0][0] <= n:
-            seq.append(("M", items[0][2], items[0][1]))
-            items = items[1:]
-    for it in items:
-        seq.append(("M", it[2], it[1]))
-    return seq
+            if h == 1 and i >= 4:
+                continue
+            for s in range(SLICES):
+                ready = max([chunk_of("X", i, s)] + [chunk_of("W", 4 * h + j, s) for j in range(4)])
+                blocks.append((ready, h, i, s))
+    return sorted(blocks)
 
 
 def tile_fftmlp_kernel(tc, x, filters_real, filters_imag, out):
@@ -56,8 +54,8 @@ def tile_fftmlp_kernel(tc, x, filters_real, filters_imag, out):
     with ExitStack() as ctx:
         keep = ctx.enter_context(tc.tile_pool(name="keep", bufs=1))
         raw_pool = ctx.enter_context(tc.tile_pool(name="rawp", bufs=RAW_BUFS))
-        stage_pool = ctx.enter_context(tc.tile_pool(name="stagep", bufs=STAGE_BUFS))
-        wg_pool = ctx.enter_context(tc.tile_pool(name="wgp", bufs=2))
+        perm_pool = ctx.enter_context(tc.tile_pool(name="permp", bufs=4))
+        stage_pool = ctx.enter_context(tc.tile_pool(name="stagep", bufs=8))
         res_pool = ctx.enter_context(tc.tile_pool(name="resp", bufs=4))
         tp_pool = ctx.enter_context(tc.psum_pool(name="tpp", bufs=4))
         acc_pool = ctx.enter_context(tc.psum_pool(name="accp", bufs=4))
@@ -65,30 +63,130 @@ def tile_fftmlp_kernel(tc, x, filters_real, filters_imag, out):
 
         warm = keep.tile([P, 512], BF16, name="warm")
         nc.vector.memset(warm[:], 0.0)
+        table = keep.tile([P, 16], F32, name="table")
+        nc.scalar.copy(out=table[:], in_=warm[:, 0:16])
         ident = keep.tile([P, P], F32, name="ident")
         make_identity(nc, ident[:])
 
-        x_codes = [keep.tile([P, PASSES * P], U32, name="xc%d" % i, align_bytes=64) for i in range(B // P)]
-        x_scales = [keep.tile([P, PASSES * P], U8, name="xs%d" % i, align_bytes=64) for i in range(B // P)]
-        w_codes = [keep.tile([P, PASSES, NCOL], U32, name="wc%d" % j, align_bytes=64) for j in range(O // NCOL)]
-        w_scales = [keep.tile([P, PASSES, NCOL], U8, name="ws%d" % j, align_bytes=64) for j in range(O // NCOL)]
+        x_codes = [keep.tile([P, PASSES, P], U32, name="xc%d" % i, align_bytes=64) for i in range(B // P)]
+        x_scales = [keep.tile([P, PASSES, P], U8, name="xs%d" % i, align_bytes=64) for i in range(B // P)]
+        w_codes = [keep.tile([P, PASSES, HALF], U32, name="wc%d" % h, align_bytes=64) for h in range(2)]
+        w_scales = [keep.tile([P, PASSES, HALF], U8, name="ws%d" % h, align_bytes=64) for h in range(2)]
 
         raws = {}
+        perms = {}
 
         def load(n):
-            kind, idx = UNITS[n]
-            raw = raw_pool.tile([P, 2 * F], BF16, name="raw", tag="raw")
-            rows = slice(idx * P, (idx + 1) * P)
-            if kind == "X":
-                nc.sync.dma_start(out=raw[:], in_=x[rows, :, :].rearrange("m c k -> m (c k)"))
-            else:
-                cuts = 2 if n == 0 else 1
-                step = F // cuts
-                for h in range(cuts):
-                    cols = slice(h * step, (h + 1) * step)
-                    nc.sync.dma_start(out=raw[:, h * step:(h + 1) * step], in_=filters_real[rows, cols])
-                    nc.sync.dma_start(out=raw[:, F + h * step:F + (h + 1) * step], in_=filters_imag[rows, cols])
+            kind, r0, rn, s0, sn = CHUNKS[n]
+            raw = raw_pool.tile([P, 2, rn, sn * KS], BF16, name="raw", tag="raw")
+            cols = slice(s0 * KS, (s0 + sn) * KS)
+            pieces = 2 if n == 0 else 1
+            step = rn // pieces
+            for piece in range(pieces):
+                here = slice(piece * step, (piece + 1) * step)
+                rows = slice((r0 + piece * step) * P, (r0 + (piece + 1) * step) * P)
+                for c in range(2):
+                    if kind == "X":
+                        src = x[rows, c, cols]
+                    else:
+                        src = (filters_real, filters_imag)[c][rows, cols]
+                    nc.sync.dma_start(out=raw[:, c, here, :], in_=src.rearrange("(r p) k -> p r k", p=P))
             raws[n] = raw
+
+        def prepare(n):
+            kind, r0, rn, s0, sn = CHUNKS[n]
+            perm = perm_pool.tile([P, 2 * 4 * KS], BF16, name="perm", tag="perm", align_bytes=64)
+            raw = raws[n][:].rearrange("p c r k -> p (c r k)")
+            if kind == "X":
+                words = raw.bitcast(F32).rearrange("p (q u) -> p u q", u=2)
+                nc.vector.tensor_copy(out=perm[:].bitcast(F32).rearrange("p (u q) -> p u q", u=2), in_=words)
+            else:
+                pairs = raw.rearrange("p (c q u e) -> p c u q e", c=2, u=2, e=2)
+                sums = perm[:].rearrange("p (c u q e) -> p c u q e", c=2, u=2, e=2)
+                pieces = 2 if n == 0 else 1
+                step = 512 // pieces
+                for piece in range(pieces):
+                    q = slice(piece * step, (piece + 1) * step)
+                    for c in range(2):
+                        nc.vector.tensor_tensor(
+                            out=sums[:, c, :, q, :], in0=pairs[:, 0, :, q, :], in1=pairs[:, 1, :, q, :], op=(ADD, SUB)[c]
+                        )
+            perms[n] = perm
+
+        def banks_of(n):
+            kind, r0, rn, s0, sn = CHUNKS[n]
+            banks = []
+            if kind == "X":
+                for r in range(rn):
+                    for g in range(sn):
+                        q = r * sn + g
+                        first = [u * 1024 + (c * 4 + q) * P for c in range(2) for u in range(2)]
+                        i, pa = r0 + r, 2 * (s0 + g)
+                        banks.append((first, x_codes[i][:, pa:pa + 2, :], x_scales[i][:, pa:pa + 2, :]))
+            else:
+                for r in range(0, rn, 2):
+                    for g in range(sn):
+                        for c in range(2):
+                            first = [c * 1024 + u * 512 + ((r + j) * sn + g) * P for j in range(2) for u in range(2)]
+                            pa = 2 * (s0 + g) + c
+                            h, col = (r0 + r) // 4, ((r0 + r) % 4) * P
+                            cols = slice(col, col + 2 * P)
+                            banks.append((first, w_codes[h][:, pa, cols], w_scales[h][:, pa, cols]))
+            return banks
+
+        def transpose(n):
+            words = perms[n][:].bitcast(F32)
+            stages = []
+            for first, codes, scales in banks_of(n):
+                tp = tp_pool.tile([P, 512], F32, name="tp", tag="tp")
+                for t in range(4):
+                    nc.tensor.transpose(tp[:, t * P:(t + 1) * P], words[:, first[t]:first[t] + P], ident[:])
+                stage = stage_pool.tile([P, 1024], BF16, name="stage", tag="stage", align_bytes=64)
+                nc.scalar.copy(
+                    out=stage[:].bitcast(F32).rearrange("p (v m u) -> p v m u", v=2, u=2),
+                    in_=tp[:].rearrange("p (v u m) -> p v m u", v=2, u=2),
+                )
+                stages.append((stage, codes, scales))
+            return stages
+
+        def quantise(stages):
+            for stage, codes, scales in stages:
+                if len(codes.shape) == 3:
+                    codes = codes.rearrange("p a m -> p (a m)")
+                    scales = scales.rearrange("p a m -> p (a m)")
+                nc.vector.quantize_mx(out=codes.bitcast(FP8X4), scales=scales, in_=stage[:])
+
+        accs = {}
+
+        def passes(h, i, pa_list, acc, cols, first, last):
+            for pa in pa_list:
+                nc.tensor.matmul_mx(
+                    out=acc[:, cols],
+                    lhsT=x_codes[i][:, pa, :].bitcast(FP8X4),
+                    lhsT_scale=x_scales[i][:, pa, :],
+                    rhs=w_codes[h][:, pa, cols].bitcast(FP8X4),
+                    rhs_scale=w_scales[h][:, pa, cols],
+                    start=(pa == first),
+                    stop=(pa == last),
+                )
+
+        def store(h, i, acc, cols, engine):
+            res = res_pool.tile([P, HALF], F32, name="res", tag="res")
+            if engine == 0:
+                nc.scalar.copy(out=res[:, cols], in_=acc[:, cols])
+            else:
+                nc.vector.tensor_copy(out=res[:, cols], in_=acc[:, cols])
+            nc.sync.dma_start(
+                out=out[i * P:(i + 1) * P, h * HALF + cols.start:h * HALF + cols.stop], in_=res[:, cols]
+            )
+
+        def multiply_block(h, i, s):
+            if s == 0:
+                accs[(h, i)] = acc_pool.tile([P, HALF], F32, name="acc", tag="acc")
+            acc = accs[(h, i)]
+            passes(h, i, [2 * s, 2 * s + 1], acc, slice(0, HALF), 0, PASSES - 1)
+            if s == SLICES - 1:
+                store(h, i, acc, slice(0, HALF), 0)
 
         warm_ps = acc_pool.tile([P, 512], F32, name="warm_ps", tag="acc")
 
@@ -96,67 +194,30 @@ def tile_fftmlp_kernel(tc, x, filters_real, filters_imag, out):
             for d in range(count):
                 nc.tensor.matmul(out=warm_ps[:], lhsT=warm[:, 0:P], rhs=warm[:], start=True, stop=True)
 
-        def transpose_unit(n):
-            kind, idx = UNITS[n]
-            words = raws[n][:].bitcast(F32)
-            stage = stage_pool.tile([P, 2 * F], BF16, name="stage", tag="stage", align_bytes=64)
-            stage_words = stage[:].bitcast(F32)
-            for b in range(4):
-                tp = tp_pool.tile([P, 512], F32, name="tp", tag="tp")
-                if kind == "X":
-                    starts = [512 * b, 512 * b + 256]
-                else:
-                    starts = [256 * b, 1024 + 256 * b]
-                for s in range(4):
-                    first = starts[s // 2] + s % 2
-                    nc.tensor.transpose(tp[:, s * P:(s + 1) * P], words[:, first:first + 255:2], ident[:])
-                src = tp[:].rearrange("p (g u m) -> p g m u", g=2, u=2)
-                if kind == "X":
-                    dst = stage_words[:, b * 512:(b + 1) * 512].rearrange("p (g m u) -> p g m u", g=2, u=2)
-                else:
-                    dst = stage_words.rearrange("p (f c m u) -> p f c m u", f=2, c=4, u=2)[:, :, b, :, :]
-                nc.scalar.copy(out=dst, in_=src)
-            if kind == "X":
-                nc.vector.quantize_mx(out=x_codes[idx][:].bitcast(FP8X4), scales=x_scales[idx][:], in_=stage[:])
-            else:
-                wg = wg_pool.tile([P, 2 * F], BF16, name="wg", tag="wg", align_bytes=64)
-                nc.vector.tensor_tensor(out=wg[:, 0:F], in0=stage[:, 0:F], in1=stage[:, F:2 * F], op=ADD)
-                nc.vector.tensor_tensor(out=wg[:, F:2 * F], in0=stage[:, 0:F], in1=stage[:, F:2 * F], op=SUB)
-                cols = slice((idx % 2) * P, (idx % 2 + 1) * P)
-                for g in range(PASSES):
-                    nc.vector.quantize_mx(
-                        out=w_codes[idx // 2][:, g, cols].bitcast(FP8X4),
-                        scales=w_scales[idx // 2][:, g, cols],
-                        in_=wg[:, g * 512:(g + 1) * 512],
-                    )
-
-        def multiply(i, j):
-            acc = acc_pool.tile([P, 512], F32, name="acc", tag="acc")
-            for g in range(PASSES):
-                nc.tensor.matmul_mx(
-                    out=acc[:, 0:NCOL],
-                    lhsT=x_codes[i][:, g * P:(g + 1) * P].bitcast(FP8X4),
-                    lhsT_scale=x_scales[i][:, g * P:(g + 1) * P],
-                    rhs=w_codes[j][:, g, :].bitcast(FP8X4),
-                    rhs_scale=w_scales[j][:, g, :],
-                    start=(g == 0),
-                    stop=(g == PASSES - 1),
-                )
-            res = res_pool.tile([P, NCOL], F32, name="res", tag="res")
-            nc.scalar.copy(out=res[:], in_=acc[:, 0:NCOL])
-            nc.sync.dma_start(out=out[i * P:(i + 1) * P, j * NCOL:(j + 1) * NCOL], in_=res[:])
-
         for n in range(RAW_BUFS):
             load(n)
-        loaded = RAW_BUFS
         warm_up(WARM_FIRST)
-        for step in pe_sequence():
-            if step[0] == "T":
-                transpose_unit(step[1])
-                if step[1] < WARM_UNITS:
-                    warm_up(WARM_EACH)
-                if loaded < len(UNITS):
-                    load(loaded)
-                    loaded += 1
-            else:
-                multiply(step[1], step[2])
+        prepare(0)
+        blocks = ready_blocks()
+        for n in range(len(CHUNKS)):
+            if n + 1 < len(CHUNKS):
+                prepare(n + 1)
+            if n + RAW_BUFS < len(CHUNKS):
+                load(n + RAW_BUFS)
+            stages = transpose(n)
+            if n < WARM_CHUNKS:
+                warm_up(WARM_EACH)
+            quantise(stages)
+            for count in range(2 if n < 6 else 4):
+                if blocks and blocks[0][0] < n:
+                    multiply_block(blocks[0][1], blocks[0][2], blocks[0][3])
+                    blocks = blocks[1:]
+        for ready, h, i, s in blocks:
+            multiply_block(h, i, s)
+        for i in range(4, 8):
+            acc = acc_pool.tile([P, HALF], F32, name="acc", tag="acc")
+            width = HALF if i < 7 else HALF // 2
+            for c0 in range(0, HALF, width):
+                cols = slice(c0, c0 + width)
+                passes(1, i, range(PASSES), acc, cols, 0, PASSES - 1)
+                store(1, i, acc, cols, (c0 // width) % 2)

@@ -22,9 +22,10 @@ HALF = 512
 CHUNKS = (
     ("W", 0, 4, 0, 1), ("X", 0, 4, 0, 1), ("W", 0, 4, 1, 1), ("X", 0, 4, 1, 1),
     ("W", 0, 2, 2, 2), ("W", 2, 2, 2, 2), ("X", 0, 2, 2, 2), ("X", 2, 2, 2, 2),
-    ("X", 4, 2, 0, 2), ("X", 6, 2, 0, 2), ("X", 4, 2, 2, 2), ("X", 6, 2, 2, 2),
     ("W", 4, 4, 0, 1), ("W", 4, 4, 1, 1), ("W", 4, 4, 2, 1), ("W", 4, 4, 3, 1),
+    ("X", 4, 2, 0, 2), ("X", 4, 2, 2, 2),
 )
+TURNED = (6, 7)
 RAW_BUFS = 10
 WARM_FIRST = 6
 WARM_EACH = 2
@@ -40,9 +41,7 @@ def chunk_of(kind, row, s):
 def ready_blocks():
     blocks = []
     for h in range(2):
-        for i in range(B // P):
-            if h == 1 and i >= 4:
-                continue
+        for i in range(TURNED[0]):
             for s in range(SLICES):
                 ready = max([chunk_of("X", i, s)] + [chunk_of("W", 4 * h + j, s) for j in range(4)])
                 blocks.append((ready, h, i, s))
@@ -75,6 +74,51 @@ def tile_fftmlp_kernel(tc, x, filters_real, filters_imag, out):
 
         raws = {}
         perms = {}
+        turned = {}
+
+        def x_pass(i, pa):
+            return (pa % 2) * SLICES + pa // 2 if i in TURNED else pa
+
+        def load_spread(i):
+            raw = raw_pool.tile([P, PASSES, 4, P], BF16, name="raw", tag="raw")
+            for g in range(4):
+                rows = x[i * P + 32 * g:i * P + 32 * (g + 1), :, :].rearrange("r c (s q k) -> q r (c s) k", q=4, k=P)
+                for q in range(4):
+                    nc.sync.dma_start(out=raw[32 * q:32 * (q + 1), :, g, :], in_=rows[q])
+            raws[("spread", i)] = raw
+
+        def separate(i):
+            words = raws[("spread", i)][:].rearrange("p s g k -> p (s g k)").bitcast(F32)
+            perm = perm_pool.tile([P, 2 * 4 * KS], BF16, name="perm", tag="perm", align_bytes=64)
+            for c in range(2):
+                half = slice(c * 1024, (c + 1) * 1024)
+                nc.vector.tensor_copy(
+                    out=perm[:].bitcast(F32)[:, half].rearrange("p (u n) -> p u n", u=2),
+                    in_=words[:, half].rearrange("p (n u) -> p u n", u=2),
+                )
+            perms[("spread", i)] = perm
+
+        def turn(i):
+            perm = perms[("spread", i)]
+            tile = perm_pool.tile([P, 2 * 4 * KS], BF16, name="turn", tag="perm", align_bytes=64)
+            for c in range(2):
+                half = slice(c * 1024, (c + 1) * 1024)
+                nc.vector.transpose(out=tile[:].bitcast(F32)[:, half], in_=perm[:].bitcast(F32)[:, half])
+            turned[i] = tile
+
+        def interleave(i):
+            stages = []
+            for c in range(2):
+                words = turned[i][:].bitcast(F32)[:, c * 1024:(c + 1) * 1024].rearrange("p (u m) -> p m u", u=2)
+                for h in range(2):
+                    stage = stage_pool.tile([P, 1024], BF16, name="stage", tag="stage", align_bytes=64)
+                    nc.scalar.copy(
+                        out=stage[:].bitcast(F32).rearrange("p (m u) -> p m u", u=2),
+                        in_=words[:, h * 2 * P:(h + 1) * 2 * P, :],
+                    )
+                    pa = c * SLICES + 2 * h
+                    stages.append((stage, x_codes[i][:, pa:pa + 2, :], x_scales[i][:, pa:pa + 2, :]))
+            return stages
 
         def load(n):
             kind, r0, rn, s0, sn = CHUNKS[n]
@@ -162,8 +206,8 @@ def tile_fftmlp_kernel(tc, x, filters_real, filters_imag, out):
             for pa in pa_list:
                 nc.tensor.matmul_mx(
                     out=acc[:, cols],
-                    lhsT=x_codes[i][:, pa, :].bitcast(FP8X4),
-                    lhsT_scale=x_scales[i][:, pa, :],
+                    lhsT=x_codes[i][:, x_pass(i, pa), :].bitcast(FP8X4),
+                    lhsT_scale=x_scales[i][:, x_pass(i, pa), :],
                     rhs=w_codes[h][:, pa, cols].bitcast(FP8X4),
                     rhs_scale=w_scales[h][:, pa, cols],
                     start=(pa == first),
@@ -194,16 +238,30 @@ def tile_fftmlp_kernel(tc, x, filters_real, filters_imag, out):
             for d in range(count):
                 nc.tensor.matmul(out=warm_ps[:], lhsT=warm[:, 0:P], rhs=warm[:], start=True, stop=True)
 
+        def whole_group(h, i, width):
+            for c0 in range(0, HALF, width):
+                acc = acc_pool.tile([P, HALF], F32, name="acc", tag="acc")
+                cols = slice(c0, c0 + width)
+                passes(h, i, range(PASSES), acc, cols, 0, PASSES - 1)
+                store(h, i, acc, cols, (c0 // width) % 2)
+
         for n in range(RAW_BUFS):
             load(n)
         warm_up(WARM_FIRST)
         prepare(0)
         blocks = ready_blocks()
+        last = len(CHUNKS) - 1
         for n in range(len(CHUNKS)):
-            if n + 1 < len(CHUNKS):
+            if n < last:
                 prepare(n + 1)
             if n + RAW_BUFS < len(CHUNKS):
                 load(n + RAW_BUFS)
+            elif n + RAW_BUFS < len(CHUNKS) + len(TURNED):
+                load_spread(TURNED[n + RAW_BUFS - len(CHUNKS)])
+            if n == last - 1:
+                separate(TURNED[0])
+            if n == last:
+                turn(TURNED[0])
             stages = transpose(n)
             if n < WARM_CHUNKS:
                 warm_up(WARM_EACH)
@@ -212,12 +270,15 @@ def tile_fftmlp_kernel(tc, x, filters_real, filters_imag, out):
                 if blocks and blocks[0][0] < n:
                     multiply_block(blocks[0][1], blocks[0][2], blocks[0][3])
                     blocks = blocks[1:]
-        for ready, h, i, s in blocks:
+        stages = interleave(TURNED[0])
+        separate(TURNED[1])
+        quantise(stages)
+        turn(TURNED[1])
+        for ready, h, i, s in blocks[:-2 * SLICES]:
             multiply_block(h, i, s)
-        for i in range(4, 8):
-            acc = acc_pool.tile([P, HALF], F32, name="acc", tag="acc")
-            width = HALF if i < 7 else HALF // 2
-            for c0 in range(0, HALF, width):
-                cols = slice(c0, c0 + width)
-                passes(1, i, range(PASSES), acc, cols, 0, PASSES - 1)
-                store(1, i, acc, cols, (c0 // width) % 2)
+        quantise(interleave(TURNED[1]))
+        for ready, h, i, s in blocks[-2 * SLICES:]:
+            multiply_block(h, i, s)
+        for i in TURNED:
+            for h in range(2):
+                whole_group(h, i, HALF // 2 if (h, i) == (1, TURNED[-1]) else HALF)

@@ -20,20 +20,32 @@ PASSES = 2 * SLICES
 HALF = 512
 
 CHUNKS = (
-    ("W", 0, 4, 0, 1), ("X", 0, 4, 0, 1), ("W", 0, 4, 1, 1), ("X", 0, 4, 1, 1),
-    ("W", 0, 2, 2, 2), ("W", 2, 2, 2, 2), ("X", 0, 2, 2, 2), ("X", 2, 2, 2, 2),
-    ("W", 4, 4, 0, 1), ("W", 4, 4, 1, 1), ("W", 4, 4, 2, 1), ("W", 4, 4, 3, 1),
-    ("X", 4, 2, 0, 2), ("X", 4, 2, 2, 2),
+    ("W", 0, 2, 0, 2, "V"),
+    ("X", 0, 2, 0, 2, "T"),
+    ("W", 2, 2, 0, 2, "V"),
+    ("X", 2, 2, 0, 2, "T"),
+    ("W", 0, 2, 2, 2, "V"),
+    ("W", 2, 2, 2, 2, "V"),
+    ("X", 0, 2, 2, 2, "T"),
+    ("X", 2, 2, 2, 2, "T"),
+    ("W", 4, 4, 0, 1, "V"),
+    ("W", 4, 4, 1, 1, "V"),
+    ("W", 4, 4, 2, 1, "V"),
+    ("W", 4, 4, 3, 1, "V"),
+    ("X", 4, 2, 0, 2, "V"),
+    ("X", 4, 2, 2, 2, "V"),
+    ("X", 6, 1, 0, 4, "V"),
 )
-TURNED = (6, 7)
+TURNED = (7,)
 RAW_BUFS = 10
 WARM_FIRST = 6
 WARM_EACH = 2
+XPIECES = 1
 WARM_CHUNKS = 2
 
 
 def chunk_of(kind, row, s):
-    for n, (k, r0, rn, s0, sn) in enumerate(CHUNKS):
+    for n, (k, r0, rn, s0, sn, mode) in enumerate(CHUNKS):
         if k == kind and r0 <= row < r0 + rn and s0 <= s < s0 + sn:
             return n
 
@@ -41,7 +53,7 @@ def chunk_of(kind, row, s):
 def ready_blocks():
     blocks = []
     for h in range(2):
-        for i in range(TURNED[0]):
+        for i in range(B // P - len(TURNED)):
             for s in range(SLICES):
                 ready = max([chunk_of("X", i, s)] + [chunk_of("W", 4 * h + j, s) for j in range(4)])
                 blocks.append((ready, h, i, s))
@@ -55,7 +67,7 @@ def tile_fftmlp_kernel(tc, x, filters_real, filters_imag, out):
         raw_pool = ctx.enter_context(tc.tile_pool(name="rawp", bufs=RAW_BUFS))
         perm_pool = ctx.enter_context(tc.tile_pool(name="permp", bufs=4))
         stage_pool = ctx.enter_context(tc.tile_pool(name="stagep", bufs=8))
-        res_pool = ctx.enter_context(tc.tile_pool(name="resp", bufs=4))
+        res_pool = ctx.enter_context(tc.tile_pool(name="resp", bufs=8))
         tp_pool = ctx.enter_context(tc.psum_pool(name="tpp", bufs=4))
         acc_pool = ctx.enter_context(tc.psum_pool(name="accp", bufs=4))
         ctx.enter_context(tc.manual_schedule())
@@ -121,7 +133,7 @@ def tile_fftmlp_kernel(tc, x, filters_real, filters_imag, out):
             return stages
 
         def load(n):
-            kind, r0, rn, s0, sn = CHUNKS[n]
+            kind, r0, rn, s0, sn, mode = CHUNKS[n]
             raw = raw_pool.tile([P, 2, rn, sn * KS], BF16, name="raw", tag="raw")
             cols = slice(s0 * KS, (s0 + sn) * KS)
             pieces = 2 if n == 0 else 1
@@ -138,12 +150,21 @@ def tile_fftmlp_kernel(tc, x, filters_real, filters_imag, out):
             raws[n] = raw
 
         def prepare(n):
-            kind, r0, rn, s0, sn = CHUNKS[n]
+            kind, r0, rn, s0, sn, mode = CHUNKS[n]
+            if mode == "T":
+                return
             perm = perm_pool.tile([P, 2 * 4 * KS], BF16, name="perm", tag="perm", align_bytes=64)
             raw = raws[n][:].rearrange("p c r k -> p (c r k)")
             if kind == "X":
                 words = raw.bitcast(F32).rearrange("p (q u) -> p u q", u=2)
-                nc.vector.tensor_copy(out=perm[:].bitcast(F32).rearrange("p (u q) -> p u q", u=2), in_=words)
+                pieces = XPIECES if mode == "V" else 2
+                for piece in range(pieces):
+                    q = slice(piece * 1024 // pieces, (piece + 1) * 1024 // pieces)
+                    dst = perm[:].bitcast(F32).rearrange("p (u q) -> p u q", u=2)[:, :, q]
+                    if mode == "V":
+                        nc.vector.tensor_copy(out=dst, in_=words[:, :, q])
+                    else:
+                        nc.scalar.copy(out=dst, in_=words[:, :, q])
             else:
                 pairs = raw.rearrange("p (c q u e) -> p c u q e", c=2, u=2, e=2)
                 sums = perm[:].rearrange("p (c u q e) -> p c u q e", c=2, u=2, e=2)
@@ -158,13 +179,16 @@ def tile_fftmlp_kernel(tc, x, filters_real, filters_imag, out):
             perms[n] = perm
 
         def banks_of(n):
-            kind, r0, rn, s0, sn = CHUNKS[n]
+            kind, r0, rn, s0, sn, mode = CHUNKS[n]
             banks = []
             if kind == "X":
                 for r in range(rn):
                     for g in range(sn):
                         q = r * sn + g
-                        first = [u * 1024 + (c * 4 + q) * P for c in range(2) for u in range(2)]
+                        if mode == "T":
+                            first = [(c * 4 + q) * 2 * P + u for c in range(2) for u in range(2)]
+                        else:
+                            first = [u * 1024 + (c * 4 + q) * P for c in range(2) for u in range(2)]
                         i, pa = r0 + r, 2 * (s0 + g)
                         banks.append((first, x_codes[i][:, pa:pa + 2, :], x_scales[i][:, pa:pa + 2, :]))
             else:
@@ -179,12 +203,17 @@ def tile_fftmlp_kernel(tc, x, filters_real, filters_imag, out):
             return banks
 
         def transpose(n):
-            words = perms[n][:].bitcast(F32)
+            step = 1
+            if CHUNKS[n][5] == "T":
+                words = raws[n][:].rearrange("p c r k -> p (c r k)").bitcast(F32)
+                step = 2
+            else:
+                words = perms[n][:].bitcast(F32)
             stages = []
             for first, codes, scales in banks_of(n):
                 tp = tp_pool.tile([P, 512], F32, name="tp", tag="tp")
                 for t in range(4):
-                    nc.tensor.transpose(tp[:, t * P:(t + 1) * P], words[:, first[t]:first[t] + P], ident[:])
+                    nc.tensor.transpose(tp[:, t * P:(t + 1) * P], words[:, first[t]:first[t] + step * (P - 1) + 1:step], ident[:])
                 stage = stage_pool.tile([P, 1024], BF16, name="stage", tag="stage", align_bytes=64)
                 nc.scalar.copy(
                     out=stage[:].bitcast(F32).rearrange("p (v m u) -> p v m u", v=2, u=2),
@@ -252,7 +281,8 @@ def tile_fftmlp_kernel(tc, x, filters_real, filters_imag, out):
         blocks = ready_blocks()
         last = len(CHUNKS) - 1
         for n in range(len(CHUNKS)):
-            if n < last:
+            early = n < 0
+            if n < last and CHUNKS[n + 1][5] != "S" and not early:
                 prepare(n + 1)
             if n + RAW_BUFS < len(CHUNKS):
                 load(n + RAW_BUFS)
@@ -265,19 +295,18 @@ def tile_fftmlp_kernel(tc, x, filters_real, filters_imag, out):
             stages = transpose(n)
             if n < WARM_CHUNKS:
                 warm_up(WARM_EACH)
+            if n < last and CHUNKS[n + 1][5] == "S" and not early:
+                prepare(n + 1)
             quantise(stages)
-            for count in range(2 if n < 6 else 4):
+            if n < last and early:
+                prepare(n + 1)
+            for count in range(4):
                 if blocks and blocks[0][0] < n:
                     multiply_block(blocks[0][1], blocks[0][2], blocks[0][3])
                     blocks = blocks[1:]
         stages = interleave(TURNED[0])
-        separate(TURNED[1])
         quantise(stages)
-        turn(TURNED[1])
-        for ready, h, i, s in blocks[:-2 * SLICES]:
-            multiply_block(h, i, s)
-        quantise(interleave(TURNED[1]))
-        for ready, h, i, s in blocks[-2 * SLICES:]:
+        for ready, h, i, s in blocks:
             multiply_block(h, i, s)
         for i in TURNED:
             for h in range(2):

@@ -32,13 +32,11 @@ CHUNKS = (
     ("W", 4, 4, 1, 1, "V"),
     ("W", 4, 4, 2, 1, "V"),
     ("W", 4, 4, 3, 1, "V"),
-    ("X", 4, 2, 0, 2, "V"),
-    ("X", 4, 2, 2, 2, "V"),
-    ("X", 6, 1, 0, 4, "V"),
+    ("X", 4, 1, 0, 4, "V"),
 )
-TURNED = (7,)
+TURNED = (5, 6, 7)
 RAW_BUFS = 10
-WARM_FIRST = 6
+WARM_FIRST = 8
 WARM_EACH = 2
 XPIECES = 1
 WARM_CHUNKS = 2
@@ -300,14 +298,26 @@ def tile_fftmlp_kernel(tc, x, filters_real, filters_imag, out):
             quantise(stages)
             if n < last and early:
                 prepare(n + 1)
-            for count in range(4):
+            for count in range(2 if n < 8 else 4):
                 if blocks and blocks[0][0] < n:
                     multiply_block(blocks[0][1], blocks[0][2], blocks[0][3])
                     blocks = blocks[1:]
         stages = interleave(TURNED[0])
+        for t in range(1, len(TURNED)):
+            separate(TURNED[t])
+            quantise(stages)
+            turn(TURNED[t])
+            if t == 1:
+                for ready, h, i, s in blocks[:-2 * SLICES]:
+                    multiply_block(h, i, s)
+            else:
+                for h in range(2):
+                    whole_group(h, TURNED[t - 2], HALF)
+            stages = interleave(TURNED[t])
+            if t == 1:
+                for ready, h, i, s in blocks[-2 * SLICES:]:
+                    multiply_block(h, i, s)
         quantise(stages)
-        for ready, h, i, s in blocks:
-            multiply_block(h, i, s)
-        for i in TURNED:
+        for i in TURNED[-2:]:
             for h in range(2):
                 whole_group(h, i, HALF // 2 if (h, i) == (1, TURNED[-1]) else HALF)

@@ -25,8 +25,8 @@ CHUNKS = (
     ("W", 2, 2, 0, 2, "V"),
     ("X", 2, 2, 0, 2, "T"),
     ("W", 0, 2, 2, 2, "V"),
-    ("W", 2, 2, 2, 2, "V"),
     ("X", 0, 2, 2, 2, "T"),
+    ("W", 2, 2, 2, 2, "V"),
     ("X", 2, 2, 2, 2, "T"),
     ("W", 4, 4, 0, 1, "V"),
     ("W", 4, 4, 1, 1, "V"),
@@ -134,7 +134,7 @@ def tile_fftmlp_kernel(tc, x, filters_real, filters_imag, out):
             kind, r0, rn, s0, sn, mode = CHUNKS[n]
             raw = raw_pool.tile([P, 2, rn, sn * KS], BF16, name="raw", tag="raw")
             cols = slice(s0 * KS, (s0 + sn) * KS)
-            pieces = 2 if n == 0 else 1
+            pieces = 2 if n < 4 else 1
             step = rn // pieces
             for piece in range(pieces):
                 here = slice(piece * step, (piece + 1) * step)
@@ -166,7 +166,7 @@ def tile_fftmlp_kernel(tc, x, filters_real, filters_imag, out):
             else:
                 pairs = raw.rearrange("p (c q u e) -> p c u q e", c=2, u=2, e=2)
                 sums = perm[:].rearrange("p (c u q e) -> p c u q e", c=2, u=2, e=2)
-                pieces = 2 if n == 0 else 1
+                pieces = 2 if n < 4 else 1
                 step = 512 // pieces
                 for piece in range(pieces):
                     q = slice(piece * step, (piece + 1) * step)

@@ -20,26 +20,18 @@ PASSES = 2 * SLICES
 HALF = 512
 
 CHUNKS = (
-    ("W", 0, 2, 0, 2, "V"),
-    ("X", 0, 2, 0, 2, "T"),
-    ("W", 2, 2, 0, 2, "V"),
-    ("X", 2, 2, 0, 2, "T"),
-    ("W", 0, 2, 2, 2, "V"),
-    ("X", 0, 2, 2, 2, "T"),
-    ("W", 2, 2, 2, 2, "V"),
-    ("X", 2, 2, 2, 2, "T"),
-    ("W", 4, 4, 0, 1, "V"),
-    ("W", 4, 4, 1, 1, "V"),
-    ("W", 4, 4, 2, 1, "V"),
-    ("W", 4, 4, 3, 1, "V"),
+    ("W", 0, 2, 0, 2, "V"), ("X", 0, 2, 0, 2, "V"), ("W", 2, 2, 0, 2, "V"), ("X", 2, 2, 0, 2, "V"),
+    ("W", 0, 2, 2, 2, "V"), ("X", 0, 2, 2, 2, "V"), ("W", 2, 2, 2, 2, "V"), ("X", 2, 2, 2, 2, "V"),
+    ("W", 4, 4, 0, 1, "V"), ("W", 4, 4, 1, 1, "V"), ("W", 4, 4, 2, 1, "V"), ("W", 4, 4, 3, 1, "V"),
     ("X", 4, 1, 0, 4, "V"),
 )
 TURNED = (5, 6, 7)
 RAW_BUFS = 10
 WARM_FIRST = 8
 WARM_EACH = 2
-XPIECES = 1
 WARM_CHUNKS = 2
+FIRST_PHASE = 8
+CHANNELS = {"T": (0, 1), "V": (0, 1), "H": (1, 0)}
 
 
 def chunk_of(kind, row, s):
@@ -86,9 +78,6 @@ def tile_fftmlp_kernel(tc, x, filters_real, filters_imag, out):
         perms = {}
         turned = {}
 
-        def x_pass(i, pa):
-            return (pa % 2) * SLICES + pa // 2 if i in TURNED else pa
-
         def load_spread(i):
             raw = raw_pool.tile([P, PASSES, 4, P], BF16, name="raw", tag="raw")
             for g in range(4):
@@ -103,8 +92,8 @@ def tile_fftmlp_kernel(tc, x, filters_real, filters_imag, out):
             for c in range(2):
                 half = slice(c * 1024, (c + 1) * 1024)
                 nc.vector.tensor_copy(
-                    out=perm[:].bitcast(F32)[:, half].rearrange("p (u n) -> p u n", u=2),
-                    in_=words[:, half].rearrange("p (n u) -> p u n", u=2),
+                    out=perm[:].bitcast(F32)[:, half].rearrange("p (u n f) -> p u n f", u=2, f=8),
+                    in_=words[:, half].rearrange("p (n u f) -> p u n f", u=2, f=8),
                 )
             perms[("spread", i)] = perm
 
@@ -126,8 +115,12 @@ def tile_fftmlp_kernel(tc, x, filters_real, filters_imag, out):
                         out=stage[:].bitcast(F32).rearrange("p (m u) -> p m u", u=2),
                         in_=words[:, h * 2 * P:(h + 1) * 2 * P, :],
                     )
-                    pa = c * SLICES + 2 * h
-                    stages.append((stage, x_codes[i][:, pa:pa + 2, :], x_scales[i][:, pa:pa + 2, :]))
+                    pa = slice(c * SLICES + 2 * h, c * SLICES + 2 * h + 2)
+                    stages.append((
+                        stage,
+                        x_codes[i][:, pa, :].rearrange("p a m -> p (a m)"),
+                        x_scales[i][:, pa, :].rearrange("p a m -> p (a m)"),
+                    ))
             return stages
 
         def load(n):
@@ -153,21 +146,21 @@ def tile_fftmlp_kernel(tc, x, filters_real, filters_imag, out):
                 return
             perm = perm_pool.tile([P, 2 * 4 * KS], BF16, name="perm", tag="perm", align_bytes=64)
             raw = raws[n][:].rearrange("p c r k -> p (c r k)")
-            if kind == "X":
-                words = raw.bitcast(F32).rearrange("p (q u) -> p u q", u=2)
-                pieces = XPIECES if mode == "V" else 2
-                for piece in range(pieces):
-                    q = slice(piece * 1024 // pieces, (piece + 1) * 1024 // pieces)
-                    dst = perm[:].bitcast(F32).rearrange("p (u q) -> p u q", u=2)[:, :, q]
-                    if mode == "V":
-                        nc.vector.tensor_copy(out=dst, in_=words[:, :, q])
-                    else:
-                        nc.scalar.copy(out=dst, in_=words[:, :, q])
+            if mode == "H":
+                words = raw.bitcast(F32)[:, 0:1024].rearrange("p (q u) -> p u q", u=2)
+                nc.scalar.copy(out=perm[:].bitcast(F32)[:, 0:1024].rearrange("p (u q) -> p u q", u=2), in_=words)
+            elif kind == "X":
+                for c in range(2):
+                    half = slice(c * 1024, (c + 1) * 1024)
+                    words = raw.bitcast(F32)[:, half].rearrange("p (b u f) -> p u b f", u=2, f=8)
+                    nc.vector.tensor_copy(
+                        out=perm[:].bitcast(F32)[:, half].rearrange("p (u b f) -> p u b f", u=2, f=8), in_=words
+                    )
             else:
-                pairs = raw.rearrange("p (c q u e) -> p c u q e", c=2, u=2, e=2)
-                sums = perm[:].rearrange("p (c u q e) -> p c u q e", c=2, u=2, e=2)
+                pairs = raw.rearrange("p (c b u f) -> p c u b f", c=2, u=2, f=16)
+                sums = perm[:].rearrange("p (c u b f) -> p c u b f", c=2, u=2, f=16)
                 pieces = 2 if n < 4 else 1
-                step = 512 // pieces
+                step = 64 // pieces
                 for piece in range(pieces):
                     q = slice(piece * step, (piece + 1) * step)
                     for c in range(2):
@@ -180,38 +173,47 @@ def tile_fftmlp_kernel(tc, x, filters_real, filters_imag, out):
             kind, r0, rn, s0, sn, mode = CHUNKS[n]
             banks = []
             if kind == "X":
-                for r in range(rn):
-                    for g in range(sn):
-                        q = r * sn + g
-                        if mode == "T":
-                            first = [(c * 4 + q) * 2 * P + u for c in range(2) for u in range(2)]
-                        else:
-                            first = [u * 1024 + (c * 4 + q) * P for c in range(2) for u in range(2)]
-                        i, pa = r0 + r, 2 * (s0 + g)
-                        banks.append((first, x_codes[i][:, pa:pa + 2, :], x_scales[i][:, pa:pa + 2, :]))
+                raw_words = raws[n][:].rearrange("p c r k -> p (c r k)").bitcast(F32)
+                for c in CHANNELS[mode]:
+                    for r in range(rn):
+                        for g in range(0, sn, 2):
+                            q = r * sn + g
+                            views = []
+                            for d in range(2):
+                                for u in range(2):
+                                    if mode == "T" or (mode == "H" and c == 1):
+                                        first = (c * 4 + q + d) * 2 * P + u
+                                        views.append(raw_words[:, first:first + 2 * P - 1:2])
+                                    else:
+                                        first = c * 1024 + u * 512 + (q + d) * P
+                                        views.append(perms[n][:].bitcast(F32)[:, first:first + P])
+                            i, pa = r0 + r, slice(c * SLICES + s0 + g, c * SLICES + s0 + g + 2)
+                            banks.append((
+                                views,
+                                x_codes[i][:, pa, :].rearrange("p a m -> p (a m)"),
+                                x_scales[i][:, pa, :].rearrange("p a m -> p (a m)"),
+                            ))
             else:
                 for r in range(0, rn, 2):
                     for g in range(sn):
                         for c in range(2):
-                            first = [c * 1024 + u * 512 + ((r + j) * sn + g) * P for j in range(2) for u in range(2)]
+                            views = []
+                            for d in range(2):
+                                for u in range(2):
+                                    first = c * 1024 + u * 512 + ((r + d) * sn + g) * P
+                                    views.append(perms[n][:].bitcast(F32)[:, first:first + P])
                             pa = 2 * (s0 + g) + c
                             h, col = (r0 + r) // 4, ((r0 + r) % 4) * P
                             cols = slice(col, col + 2 * P)
-                            banks.append((first, w_codes[h][:, pa, cols], w_scales[h][:, pa, cols]))
+                            banks.append((views, w_codes[h][:, pa, cols], w_scales[h][:, pa, cols]))
             return banks
 
         def transpose(n):
-            step = 1
-            if CHUNKS[n][5] == "T":
-                words = raws[n][:].rearrange("p c r k -> p (c r k)").bitcast(F32)
-                step = 2
-            else:
-                words = perms[n][:].bitcast(F32)
             stages = []
-            for first, codes, scales in banks_of(n):
+            for views, codes, scales in banks_of(n):
                 tp = tp_pool.tile([P, 512], F32, name="tp", tag="tp")
                 for t in range(4):
-                    nc.tensor.transpose(tp[:, t * P:(t + 1) * P], words[:, first[t]:first[t] + step * (P - 1) + 1:step], ident[:])
+                    nc.tensor.transpose(tp[:, t * P:(t + 1) * P], views[t], ident[:])
                 stage = stage_pool.tile([P, 1024], BF16, name="stage", tag="stage", align_bytes=64)
                 nc.scalar.copy(
                     out=stage[:].bitcast(F32).rearrange("p (v m u) -> p v m u", v=2, u=2),
@@ -222,23 +224,21 @@ def tile_fftmlp_kernel(tc, x, filters_real, filters_imag, out):
 
         def quantise(stages):
             for stage, codes, scales in stages:
-                if len(codes.shape) == 3:
-                    codes = codes.rearrange("p a m -> p (a m)")
-                    scales = scales.rearrange("p a m -> p (a m)")
                 nc.vector.quantize_mx(out=codes.bitcast(FP8X4), scales=scales, in_=stage[:])
 
         accs = {}
 
-        def passes(h, i, pa_list, acc, cols, first, last):
+        def passes(h, i, pa_list, acc, cols):
             for pa in pa_list:
+                xa = (pa % 2) * SLICES + pa // 2
                 nc.tensor.matmul_mx(
                     out=acc[:, cols],
-                    lhsT=x_codes[i][:, x_pass(i, pa), :].bitcast(FP8X4),
-                    lhsT_scale=x_scales[i][:, x_pass(i, pa), :],
+                    lhsT=x_codes[i][:, xa, :].bitcast(FP8X4),
+                    lhsT_scale=x_scales[i][:, xa, :],
                     rhs=w_codes[h][:, pa, cols].bitcast(FP8X4),
                     rhs_scale=w_scales[h][:, pa, cols],
-                    start=(pa == first),
-                    stop=(pa == last),
+                    start=(pa == 0),
+                    stop=(pa == PASSES - 1),
                 )
 
         def store(h, i, acc, cols, engine):
@@ -255,22 +255,22 @@ def tile_fftmlp_kernel(tc, x, filters_real, filters_imag, out):
             if s == 0:
                 accs[(h, i)] = acc_pool.tile([P, HALF], F32, name="acc", tag="acc")
             acc = accs[(h, i)]
-            passes(h, i, [2 * s, 2 * s + 1], acc, slice(0, HALF), 0, PASSES - 1)
+            passes(h, i, [2 * s, 2 * s + 1], acc, slice(0, HALF))
             if s == SLICES - 1:
                 store(h, i, acc, slice(0, HALF), 0)
+
+        def whole_group(h, i, width):
+            for c0 in range(0, HALF, width):
+                acc = acc_pool.tile([P, HALF], F32, name="acc", tag="acc")
+                cols = slice(c0, c0 + width)
+                passes(h, i, range(PASSES), acc, cols)
+                store(h, i, acc, cols, (c0 // width) % 2)
 
         warm_ps = acc_pool.tile([P, 512], F32, name="warm_ps", tag="acc")
 
         def warm_up(count):
             for d in range(count):
                 nc.tensor.matmul(out=warm_ps[:], lhsT=warm[:, 0:P], rhs=warm[:], start=True, stop=True)
-
-        def whole_group(h, i, width):
-            for c0 in range(0, HALF, width):
-                acc = acc_pool.tile([P, HALF], F32, name="acc", tag="acc")
-                cols = slice(c0, c0 + width)
-                passes(h, i, range(PASSES), acc, cols, 0, PASSES - 1)
-                store(h, i, acc, cols, (c0 // width) % 2)
 
         for n in range(RAW_BUFS):
             load(n)
@@ -279,8 +279,7 @@ def tile_fftmlp_kernel(tc, x, filters_real, filters_imag, out):
         blocks = ready_blocks()
         last = len(CHUNKS) - 1
         for n in range(len(CHUNKS)):
-            early = n < 0
-            if n < last and CHUNKS[n + 1][5] != "S" and not early:
+            if n < last and CHUNKS[n + 1][5] != "H":
                 prepare(n + 1)
             if n + RAW_BUFS < len(CHUNKS):
                 load(n + RAW_BUFS)
@@ -293,31 +292,28 @@ def tile_fftmlp_kernel(tc, x, filters_real, filters_imag, out):
             stages = transpose(n)
             if n < WARM_CHUNKS:
                 warm_up(WARM_EACH)
-            if n < last and CHUNKS[n + 1][5] == "S" and not early:
+            if n < last and CHUNKS[n + 1][5] == "H":
                 prepare(n + 1)
             quantise(stages)
-            if n < last and early:
-                prepare(n + 1)
-            for count in range(2 if n < 8 else 4):
+            for count in range(2 if n < FIRST_PHASE else 4):
                 if blocks and blocks[0][0] < n:
                     multiply_block(blocks[0][1], blocks[0][2], blocks[0][3])
                     blocks = blocks[1:]
         stages = interleave(TURNED[0])
-        for t in range(1, len(TURNED)):
-            separate(TURNED[t])
-            quantise(stages)
-            turn(TURNED[t])
-            if t == 1:
-                for ready, h, i, s in blocks[:-2 * SLICES]:
-                    multiply_block(h, i, s)
-            else:
-                for h in range(2):
-                    whole_group(h, TURNED[t - 2], HALF)
-            stages = interleave(TURNED[t])
-            if t == 1:
-                for ready, h, i, s in blocks[-2 * SLICES:]:
-                    multiply_block(h, i, s)
+        separate(TURNED[1])
         quantise(stages)
-        for i in TURNED[-2:]:
+        turn(TURNED[1])
+        for ready, h, i, s in blocks[:-2 * SLICES]:
+            multiply_block(h, i, s)
+        stages = interleave(TURNED[1])
+        for ready, h, i, s in blocks[-2 * SLICES:]:
+            multiply_block(h, i, s)
+        separate(TURNED[2])
+        quantise(stages)
+        turn(TURNED[2])
+        for h in range(2):
+            whole_group(h, TURNED[0], HALF)
+        quantise(interleave(TURNED[2]))
+        for i in TURNED[1:]:
             for h in range(2):
                 whole_group(h, i, HALF // 2 if (h, i) == (1, TURNED[-1]) else HALF)

@@ -20,10 +20,9 @@ PASSES = 2 * SLICES
 HALF = 512
 
 CHUNKS = (
-    ("W", 0, 2, 0, 2, "V"), ("X", 0, 2, 0, 2, "V"), ("W", 2, 2, 0, 2, "V"), ("X", 2, 2, 0, 2, "V"),
-    ("W", 0, 2, 2, 2, "V"), ("X", 0, 2, 2, 2, "V"), ("W", 2, 2, 2, 2, "V"), ("X", 2, 2, 2, 2, "V"),
-    ("W", 4, 4, 0, 1, "V"), ("W", 4, 4, 1, 1, "V"), ("W", 4, 4, 2, 1, "V"), ("W", 4, 4, 3, 1, "V"),
-    ("X", 4, 1, 0, 4, "V"),
+    ("W", 0, 2, 0, 2), ("W", 2, 2, 0, 2), ("X", 0, 2, 0, 2), ("X", 2, 2, 0, 2), ("W", 0, 2, 2, 2), ("X", 0, 2, 2, 2), ("W", 2, 2, 2, 2), ("X", 2, 2, 2, 2),
+    ("W", 4, 4, 0, 1), ("W", 4, 4, 1, 1), ("W", 4, 4, 2, 1), ("W", 4, 4, 3, 1),
+    ("X", 4, 1, 0, 4),
 )
 TURNED = (5, 6, 7)
 RAW_BUFS = 10
@@ -31,11 +30,10 @@ WARM_FIRST = 8
 WARM_EACH = 2
 WARM_CHUNKS = 2
 FIRST_PHASE = 8
-CHANNELS = {"T": (0, 1), "V": (0, 1), "H": (1, 0)}
 
 
 def chunk_of(kind, row, s):
-    for n, (k, r0, rn, s0, sn, mode) in enumerate(CHUNKS):
+    for n, (k, r0, rn, s0, sn) in enumerate(CHUNKS):
         if k == kind and r0 <= row < r0 + rn and s0 <= s < s0 + sn:
             return n
 
@@ -124,7 +122,7 @@ def tile_fftmlp_kernel(tc, x, filters_real, filters_imag, out):
             return stages
 
         def load(n):
-            kind, r0, rn, s0, sn, mode = CHUNKS[n]
+            kind, r0, rn, s0, sn = CHUNKS[n]
             raw = raw_pool.tile([P, 2, rn, sn * KS], BF16, name="raw", tag="raw")
             cols = slice(s0 * KS, (s0 + sn) * KS)
             pieces = 2 if n < 4 else 1
@@ -141,20 +139,15 @@ def tile_fftmlp_kernel(tc, x, filters_real, filters_imag, out):
             raws[n] = raw
 
         def prepare(n):
-            kind, r0, rn, s0, sn, mode = CHUNKS[n]
-            if mode == "T":
-                return
+            kind, r0, rn, s0, sn = CHUNKS[n]
             perm = perm_pool.tile([P, 2 * 4 * KS], BF16, name="perm", tag="perm", align_bytes=64)
             raw = raws[n][:].rearrange("p c r k -> p (c r k)")
-            if mode == "H":
-                words = raw.bitcast(F32)[:, 0:1024].rearrange("p (q u) -> p u q", u=2)
-                nc.scalar.copy(out=perm[:].bitcast(F32)[:, 0:1024].rearrange("p (u q) -> p u q", u=2), in_=words)
-            elif kind == "X":
+            if kind == "X":
                 for c in range(2):
                     half = slice(c * 1024, (c + 1) * 1024)
-                    words = raw.bitcast(F32)[:, half].rearrange("p (b u f) -> p u b f", u=2, f=8)
                     nc.vector.tensor_copy(
-                        out=perm[:].bitcast(F32)[:, half].rearrange("p (u b f) -> p u b f", u=2, f=8), in_=words
+                        out=perm[:].bitcast(F32)[:, half].rearrange("p (u b f) -> p u b f", u=2, f=8),
+                        in_=raw.bitcast(F32)[:, half].rearrange("p (b u f) -> p u b f", u=2, f=8),
                     )
             else:
                 pairs = raw.rearrange("p (c b u f) -> p c u b f", c=2, u=2, f=16)
@@ -170,23 +163,18 @@ def tile_fftmlp_kernel(tc, x, filters_real, filters_imag, out):
             perms[n] = perm
 
         def banks_of(n):
-            kind, r0, rn, s0, sn, mode = CHUNKS[n]
+            kind, r0, rn, s0, sn = CHUNKS[n]
+            words = perms[n][:].bitcast(F32)
             banks = []
             if kind == "X":
-                raw_words = raws[n][:].rearrange("p c r k -> p (c r k)").bitcast(F32)
-                for c in CHANNELS[mode]:
+                for c in range(2):
                     for r in range(rn):
                         for g in range(0, sn, 2):
-                            q = r * sn + g
                             views = []
                             for d in range(2):
                                 for u in range(2):
-                                    if mode == "T" or (mode == "H" and c == 1):
-                                        first = (c * 4 + q + d) * 2 * P + u
-                                        views.append(raw_words[:, first:first + 2 * P - 1:2])
-                                    else:
-                                        first = c * 1024 + u * 512 + (q + d) * P
-                                        views.append(perms[n][:].bitcast(F32)[:, first:first + P])
+                                    first = c * 1024 + u * 512 + (r * sn + g + d) * P
+                                    views.append(words[:, first:first + P])
                             i, pa = r0 + r, slice(c * SLICES + s0 + g, c * SLICES + s0 + g + 2)
                             banks.append((
                                 views,
@@ -201,7 +189,7 @@ def tile_fftmlp_kernel(tc, x, filters_real, filters_imag, out):
                             for d in range(2):
                                 for u in range(2):
                                     first = c * 1024 + u * 512 + ((r + d) * sn + g) * P
-                                    views.append(perms[n][:].bitcast(F32)[:, first:first + P])
+                                    views.append(words[:, first:first + P])
                             pa = 2 * (s0 + g) + c
                             h, col = (r0 + r) // 4, ((r0 + r) % 4) * P
                             cols = slice(col, col + 2 * P)
@@ -259,12 +247,14 @@ def tile_fftmlp_kernel(tc, x, filters_real, filters_imag, out):
             if s == SLICES - 1:
                 store(h, i, acc, slice(0, HALF), 0)
 
-        def whole_group(h, i, width):
-            for c0 in range(0, HALF, width):
+        def whole_group(h, i, widths):
+            c0 = 0
+            for w, width in enumerate(widths):
                 acc = acc_pool.tile([P, HALF], F32, name="acc", tag="acc")
                 cols = slice(c0, c0 + width)
                 passes(h, i, range(PASSES), acc, cols)
-                store(h, i, acc, cols, (c0 // width) % 2)
+                store(h, i, acc, cols, w % 2)
+                c0 += width
 
         warm_ps = acc_pool.tile([P, 512], F32, name="warm_ps", tag="acc")
 
@@ -279,7 +269,7 @@ def tile_fftmlp_kernel(tc, x, filters_real, filters_imag, out):
         blocks = ready_blocks()
         last = len(CHUNKS) - 1
         for n in range(len(CHUNKS)):
-            if n < last and CHUNKS[n + 1][5] != "H":
+            if n < last:
                 prepare(n + 1)
             if n + RAW_BUFS < len(CHUNKS):
                 load(n + RAW_BUFS)
@@ -292,8 +282,6 @@ def tile_fftmlp_kernel(tc, x, filters_real, filters_imag, out):
             stages = transpose(n)
             if n < WARM_CHUNKS:
                 warm_up(WARM_EACH)
-            if n < last and CHUNKS[n + 1][5] == "H":
-                prepare(n + 1)
             quantise(stages)
             for count in range(2 if n < FIRST_PHASE else 4):
                 if blocks and blocks[0][0] < n:
@@ -312,8 +300,8 @@ def tile_fftmlp_kernel(tc, x, filters_real, filters_imag, out):
         quantise(stages)
         turn(TURNED[2])
         for h in range(2):
-            whole_group(h, TURNED[0], HALF)
+            whole_group(h, TURNED[0], (HALF,))
         quantise(interleave(TURNED[2]))
         for i in TURNED[1:]:
             for h in range(2):
-                whole_group(h, i, HALF // 2 if (h, i) == (1, TURNED[-1]) else HALF)
+                whole_group(h, i, (256, 128, 128) if (h, i) == (1, TURNED[-1]) else (HALF,))

from contextlib import ExitStack

import concourse.mybir as mybir
from concourse.masks import make_identity

F32 = mybir.dt.float32
BF16 = mybir.dt.bfloat16
U32 = mybir.dt.uint32
U8 = mybir.dt.uint8
FP8X4 = mybir.dt.float8_e4m3fn_x4
ADD = mybir.AluOpType.add
SUB = mybir.AluOpType.subtract

P = 128
B, F, O = 1024, 2048, 1024
FLOPS = 2 * B * O * 2 * F
KS = 512
SLICES = F // KS
PASSES = 2 * SLICES
HALF = 512

CHUNKS = (
    ("W", 0, 2, 0, 2), ("W", 2, 2, 0, 2), ("X", 0, 2, 0, 2), ("X", 2, 2, 0, 2), ("W", 0, 2, 2, 2), ("X", 0, 2, 2, 2), ("W", 2, 2, 2, 2), ("X", 2, 2, 2, 2),
    ("W", 4, 4, 0, 1), ("W", 4, 4, 1, 1), ("W", 4, 4, 2, 1), ("W", 4, 4, 3, 1),
    ("X", 4, 1, 0, 4),
)
TURNED = (5, 6, 7)
RAW_BUFS = 10
WARM_FIRST = 8
WARM_EACH = 2
WARM_CHUNKS = 2
FIRST_PHASE = 8


def chunk_of(kind, row, s):
    for n, (k, r0, rn, s0, sn) in enumerate(CHUNKS):
        if k == kind and r0 <= row < r0 + rn and s0 <= s < s0 + sn:
            return n


def ready_blocks():
    blocks = []
    for h in range(2):
        for i in range(B // P - len(TURNED)):
            for s in range(SLICES):
                ready = max([chunk_of("X", i, s)] + [chunk_of("W", 4 * h + j, s) for j in range(4)])
                blocks.append((ready, h, i, s))
    return sorted(blocks)


def tile_fftmlp_kernel(tc, x, filters_real, filters_imag, out):
    nc = tc.nc
    with ExitStack() as ctx:
        keep = ctx.enter_context(tc.tile_pool(name="keep", bufs=1))
        raw_pool = ctx.enter_context(tc.tile_pool(name="rawp", bufs=RAW_BUFS))
        perm_pool = ctx.enter_context(tc.tile_pool(name="permp", bufs=4))
        stage_pool = ctx.enter_context(tc.tile_pool(name="stagep", bufs=8))
        res_pool = ctx.enter_context(tc.tile_pool(name="resp", bufs=8))
        tp_pool = ctx.enter_context(tc.psum_pool(name="tpp", bufs=4))
        acc_pool = ctx.enter_context(tc.psum_pool(name="accp", bufs=4))
        ctx.enter_context(tc.manual_schedule())

        warm = keep.tile([P, 512], BF16, name="warm")
        nc.vector.memset(warm[:], 0.0)
        table = keep.tile([P, 16], F32, name="table")
        nc.scalar.copy(out=table[:], in_=warm[:, 0:16])
        ident = keep.tile([P, P], F32, name="ident")
        make_identity(nc, ident[:])

        x_codes = [keep.tile([P, PASSES, P], U32, name="xc%d" % i, align_bytes=64) for i in range(B // P)]
        x_scales = [keep.tile([P, PASSES, P], U8, name="xs%d" % i, align_bytes=64) for i in range(B // P)]
        w_codes = [keep.tile([P, PASSES, HALF], U32, name="wc%d" % h, align_bytes=64) for h in range(2)]
        w_scales = [keep.tile([P, PASSES, HALF], U8, name="ws%d" % h, align_bytes=64) for h in range(2)]

        raws = {}
        perms = {}
        turned = {}

        def load_spread(i):
            raw = raw_pool.tile([P, PASSES, 4, P], BF16, name="raw", tag="raw")
            for g in range(4):
                rows = x[i * P + 32 * g:i * P + 32 * (g + 1), :, :].rearrange("r c (s q k) -> q r (c s) k", q=4, k=P)
                for q in range(4):
                    nc.sync.dma_start(out=raw[32 * q:32 * (q + 1), :, g, :], in_=rows[q])
            raws[("spread", i)] = raw

        def separate(i):
            words = raws[("spread", i)][:].rearrange("p s g k -> p (s g k)").bitcast(F32)
            perm = perm_pool.tile([P, 2 * 4 * KS], BF16, name="perm", tag="perm", align_bytes=64)
            for c in range(2):
                half = slice(c * 1024, (c + 1) * 1024)
                nc.vector.tensor_copy(
                    out=perm[:].bitcast(F32)[:, half].rearrange("p (u n f) -> p u n f", u=2, f=8),
                    in_=words[:, half].rearrange("p (n u f) -> p u n f", u=2, f=8),
                )
            perms[("spread", i)] = perm

        def turn(i):
            perm = perms[("spread", i)]
            tile = perm_pool.tile([P, 2 * 4 * KS], BF16, name="turn", tag="perm", align_bytes=64)
            for c in range(2):
                half = slice(c * 1024, (c + 1) * 1024)
                nc.vector.transpose(out=tile[:].bitcast(F32)[:, half], in_=perm[:].bitcast(F32)[:, half])
            turned[i] = tile

        def interleave(i):
            stages = []
            for c in range(2):
                words = turned[i][:].bitcast(F32)[:, c * 1024:(c + 1) * 1024].rearrange("p (u m) -> p m u", u=2)
                for h in range(2):
                    stage = stage_pool.tile([P, 1024], BF16, name="stage", tag="stage", align_bytes=64)
                    nc.scalar.copy(
                        out=stage[:].bitcast(F32).rearrange("p (m u) -> p m u", u=2),
                        in_=words[:, h * 2 * P:(h + 1) * 2 * P, :],
                    )
                    pa = slice(c * SLICES + 2 * h, c * SLICES + 2 * h + 2)
                    stages.append((
                        stage,
                        x_codes[i][:, pa, :].rearrange("p a m -> p (a m)"),
                        x_scales[i][:, pa, :].rearrange("p a m -> p (a m)"),
                    ))
            return stages

        def load(n):
            kind, r0, rn, s0, sn = CHUNKS[n]
            raw = raw_pool.tile([P, 2, rn, sn * KS], BF16, name="raw", tag="raw")
            cols = slice(s0 * KS, (s0 + sn) * KS)
            pieces = 2 if n < 4 else 1
            step = rn // pieces
            for piece in range(pieces):
                here = slice(piece * step, (piece + 1) * step)
                rows = slice((r0 + piece * step) * P, (r0 + (piece + 1) * step) * P)
                for c in range(2):
                    if kind == "X":
                        src = x[rows, c, cols]
                    else:
                        src = (filters_real, filters_imag)[c][rows, cols]
                    nc.sync.dma_start(out=raw[:, c, here, :], in_=src.rearrange("(r p) k -> p r k", p=P))
            raws[n] = raw

        def prepare(n):
            kind, r0, rn, s0, sn = CHUNKS[n]
            perm = perm_pool.tile([P, 2 * 4 * KS], BF16, name="perm", tag="perm", align_bytes=64)
            raw = raws[n][:].rearrange("p c r k -> p (c r k)")
            if kind == "X":
                for c in range(2):
                    half = slice(c * 1024, (c + 1) * 1024)
                    nc.vector.tensor_copy(
                        out=perm[:].bitcast(F32)[:, half].rearrange("p (u b f) -> p u b f", u=2, f=8),
                        in_=raw.bitcast(F32)[:, half].rearrange("p (b u f) -> p u b f", u=2, f=8),
                    )
            else:
                pairs = raw.rearrange("p (c b u f) -> p c u b f", c=2, u=2, f=16)
                sums = perm[:].rearrange("p (c u b f) -> p c u b f", c=2, u=2, f=16)
                pieces = 2 if n < 4 else 1
                step = 64 // pieces
                for piece in range(pieces):
                    q = slice(piece * step, (piece + 1) * step)
                    for c in range(2):
                        nc.vector.tensor_tensor(
                            out=sums[:, c, :, q, :], in0=pairs[:, 0, :, q, :], in1=pairs[:, 1, :, q, :], op=(ADD, SUB)[c]
                        )
            perms[n] = perm

        def banks_of(n):
            kind, r0, rn, s0, sn = CHUNKS[n]
            words = perms[n][:].bitcast(F32)
            banks = []
            if kind == "X":
                for c in range(2):
                    for r in range(rn):
                        for g in range(0, sn, 2):
                            views = []
                            for d in range(2):
                                for u in range(2):
                                    first = c * 1024 + u * 512 + (r * sn + g + d) * P
                                    views.append(words[:, first:first + P])
                            i, pa = r0 + r, slice(c * SLICES + s0 + g, c * SLICES + s0 + g + 2)
                            banks.append((
                                views,
                                x_codes[i][:, pa, :].rearrange("p a m -> p (a m)"),
                                x_scales[i][:, pa, :].rearrange("p a m -> p (a m)"),
                            ))
            else:
                for r in range(0, rn, 2):
                    for g in range(sn):
                        for c in range(2):
                            views = []
                            for d in range(2):
                                for u in range(2):
                                    first = c * 1024 + u * 512 + ((r + d) * sn + g) * P
                                    views.append(words[:, first:first + P])
                            pa = 2 * (s0 + g) + c
                            h, col = (r0 + r) // 4, ((r0 + r) % 4) * P
                            cols = slice(col, col + 2 * P)
                            banks.append((views, w_codes[h][:, pa, cols], w_scales[h][:, pa, cols]))
            return banks

        def transpose(n):
            stages = []
            for views, codes, scales in banks_of(n):
                tp = tp_pool.tile([P, 512], F32, name="tp", tag="tp")
                for t in range(4):
                    nc.tensor.transpose(tp[:, t * P:(t + 1) * P], views[t], ident[:])
                stage = stage_pool.tile([P, 1024], BF16, name="stage", tag="stage", align_bytes=64)
                nc.scalar.copy(
                    out=stage[:].bitcast(F32).rearrange("p (v m u) -> p v m u", v=2, u=2),
                    in_=tp[:].rearrange("p (v u m) -> p v m u", v=2, u=2),
                )
                stages.append((stage, codes, scales))
            return stages

        def quantise(stages):
            for stage, codes, scales in stages:
                nc.vector.quantize_mx(out=codes.bitcast(FP8X4), scales=scales, in_=stage[:])

        accs = {}

        def passes(h, i, pa_list, acc, cols):
            for pa in pa_list:
                xa = (pa % 2) * SLICES + pa // 2
                nc.tensor.matmul_mx(
                    out=acc[:, cols],
                    lhsT=x_codes[i][:, xa, :].bitcast(FP8X4),
                    lhsT_scale=x_scales[i][:, xa, :],
                    rhs=w_codes[h][:, pa, cols].bitcast(FP8X4),
                    rhs_scale=w_scales[h][:, pa, cols],
                    start=(pa == 0),
                    stop=(pa == PASSES - 1),
                )

        def store(h, i, acc, cols, engine):
            res = res_pool.tile([P, HALF], F32, name="res", tag="res")
            if engine == 0:
                nc.scalar.copy(out=res[:, cols], in_=acc[:, cols])
            else:
                nc.vector.tensor_copy(out=res[:, cols], in_=acc[:, cols])
            nc.sync.dma_start(
                out=out[i * P:(i + 1) * P, h * HALF + cols.start:h * HALF + cols.stop], in_=res[:, cols]
            )

        def multiply_block(h, i, s):
            if s == 0:
                accs[(h, i)] = acc_pool.tile([P, HALF], F32, name="acc", tag="acc")
            acc = accs[(h, i)]
            passes(h, i, [2 * s, 2 * s + 1], acc, slice(0, HALF))
            if s == SLICES - 1:
                store(h, i, acc, slice(0, HALF), 0)

        def whole_group(h, i, widths):
            c0 = 0
            for w, width in enumerate(widths):
                acc = acc_pool.tile([P, HALF], F32, name="acc", tag="acc")
                cols = slice(c0, c0 + width)
                passes(h, i, range(PASSES), acc, cols)
                store(h, i, acc, cols, w % 2)
                c0 += width

        warm_ps = acc_pool.tile([P, 512], F32, name="warm_ps", tag="acc")

        def warm_up(count):
            for d in range(count):
                nc.tensor.matmul(out=warm_ps[:], lhsT=warm[:, 0:P], rhs=warm[:], start=True, stop=True)

        for n in range(RAW_BUFS):
            load(n)
        warm_up(WARM_FIRST)
        prepare(0)
        blocks = ready_blocks()
        last = len(CHUNKS) - 1
        for n in range(len(CHUNKS)):
            if n < last:
                prepare(n + 1)
            if n + RAW_BUFS < len(CHUNKS):
                load(n + RAW_BUFS)
            elif n + RAW_BUFS < len(CHUNKS) + len(TURNED):
                load_spread(TURNED[n + RAW_BUFS - len(CHUNKS)])
            if n == last - 1:
                separate(TURNED[0])
            if n == last:
                turn(TURNED[0])
            stages = transpose(n)
            if n < WARM_CHUNKS:
                warm_up(WARM_EACH)
            quantise(stages)
            for count in range(2 if n < FIRST_PHASE else 4):
                if blocks and blocks[0][0] < n:
                    multiply_block(blocks[0][1], blocks[0][2], blocks[0][3])
                    blocks = blocks[1:]
        stages = interleave(TURNED[0])
        separate(TURNED[1])
        quantise(stages)
        turn(TURNED[1])
        for ready, h, i, s in blocks[:-2 * SLICES]:
            multiply_block(h, i, s)
        stages = interleave(TURNED[1])
        for ready, h, i, s in blocks[-2 * SLICES:]:
            multiply_block(h, i, s)
        separate(TURNED[2])
        quantise(stages)
        turn(TURNED[2])
        for h in range(2):
            whole_group(h, TURNED[0], (HALF,))
        quantise(interleave(TURNED[2]))
        for i in TURNED[1:]:
            for h in range(2):
                whole_group(h, i, (256, 128, 128) if (h, i) == (1, TURNED[-1]) else (HALF,))
